import numpy as np
import ml_dtypes


def mxq(x, axis, fmt="e4m3"):
    dtype, down = {"e4m3": (ml_dtypes.float8_e4m3fn, 7), "e5m2": (ml_dtypes.float8_e5m2, 14)}[fmt]
    v = np.moveaxis(np.asarray(x, np.float32).astype(ml_dtypes.bfloat16).astype(np.float64), axis, -1)
    blocks = v.reshape(v.shape[:-1] + (-1, 32))
    amax = np.abs(blocks).max(-1, keepdims=True)
    byte = np.maximum(np.where(amax > 0, np.frexp(amax)[1] - 1 + 127, 0) - down, 1)
    scale = np.exp2(byte - 127.0)
    codes = (blocks / scale).astype(np.float32).astype(dtype).astype(np.float64)
    return np.moveaxis((codes * scale).reshape(v.shape), -1, axis)


WIDE = False


def mx_kscale(k):
    if not WIDE:
        return np.ones(k)
    levels = np.array([10, -10, 5, -5, 0])
    if k % 512:
        return np.exp2(np.random.permutation(np.resize(levels, k // 32))).repeat(32)
    a = np.empty((k // 512, 16))
    for p in range(k // 512):
        a[p, :8] = np.random.permutation(np.resize(levels, 8))
        for g in range(8):
            far = levels[np.abs(levels - a[p, g]) >= 10]
            a[p, g + 8] = far[np.random.randint(len(far))]
    return np.exp2(a.ravel()).repeat(32)


BF16 = ml_dtypes.bfloat16


def bf(x):
    return np.asarray(x, np.float32).astype(BF16)


def f64(x):
    return np.asarray(x).astype(np.float64)


B, N, D, H, DH = 2, 2048, 512, 4, 64
INNER = H * DH


def dpfp(u):
    u2 = np.concatenate([np.maximum(u, 0.0), np.maximum(-u, 0.0)], axis=-1)
    return u2 * np.roll(u2, 1, axis=-1)


def heads(t):
    return t.reshape(B, N, H, DH).transpose(0, 2, 1, 3)


def setup_inputs():
    s = mx_kscale(D)
    return {"x": bf(np.random.standard_normal((B, N, D)) * s),
            "w_qk": bf(np.random.standard_normal((D, 2 * INNER)) / np.sqrt(D) / s[:, None])}


def reference(x, w_qk):
    qk = mxq(f64(x), 2, "e4m3") @ mxq(f64(w_qk), 0, "e4m3")
    q, k = np.split(qk, 2, axis=-1)
    q, k = dpfp(heads(q)), dpfp(heads(k))
    return q / q.sum(-1, keepdims=True), k / k.sum(-1, keepdims=True)

@@ -1,0 +1,244 @@
+from contextlib import ExitStack
+
+import concourse.mybir as mybir
+from concourse.masks import make_identity
+
+F32 = mybir.dt.float32
+BF16 = mybir.dt.bfloat16
+U32 = mybir.dt.uint32
+U8 = mybir.dt.uint8
+FP8X4 = mybir.dt.float8_e4m3fn_x4
+ALU = mybir.AluOpType
+ACT = mybir.ActivationFunctionType
+
+P = 128
+D = 512
+TOKENS = 4096
+SEQ = 2048
+NT = TOKENS // P
+G = 8
+DH = 64
+PADW = 68
+BLOCK_T = (2, 2, 4, 4, 4, 4, 4, 2, 2, 2, 1, 1)
+QUANT_TILES = (2, 2, 4, 8, 8, 8)
+COPY_STEP = (-1, -1, 0, 0, 1, 2, 3, 4, 6, 8, 10, 12, 14, 16, 18, 20)
+QUANT_STEP = (-1, -1, 2, 6, 14, 22)
+XT_ON_V = (1, 2, 3, 4, 5)
+NEG_ON_G = ()
+M_ON_V = (30, 31)
+OUT_LAG = 3
+
+FLOPS = 2 * TOKENS * D * D
+
+
+def tile_dpfpattention_pa_t_kernel(tc, x, w_qk, out_0, out_1):
+    nc = tc.nc
+    x_flat = x.flatten_outer_dims()
+    tile_block = []
+    tile_j = []
+    block_tile0 = []
+    for b, t_b in enumerate(BLOCK_T):
+        block_tile0.append(len(tile_block))
+        for j in range(t_b):
+            tile_block.append(b)
+            tile_j.append(j)
+    assert len(tile_block) == NT
+    q_start = [sum(QUANT_TILES[:q]) for q in range(len(QUANT_TILES))]
+    assert sum(QUANT_TILES) == NT
+    tile_q = []
+    for q, n_q in enumerate(QUANT_TILES):
+        tile_q.extend([q] * n_q)
+
+    with ExitStack() as ctx:
+        const = ctx.enter_context(tc.tile_pool(name="const", bufs=1))
+        xq = ctx.enter_context(tc.tile_pool(name="xq", bufs=2))
+        work = ctx.enter_context(tc.tile_pool(name="work", bufs=4))
+        small = ctx.enter_context(tc.tile_pool(name="small", bufs=8))
+        outp = ctx.enter_context(tc.tile_pool(name="outp", bufs=5))
+        ps_t = ctx.enter_context(tc.psum_pool(name="ps_t", bufs=2))
+        ps_a = ctx.enter_context(tc.psum_pool(name="ps_a", bufs=6))
+        ctx.enter_context(tc.manual_schedule())
+
+        w_sb = const.tile([P, 4, D], BF16)
+        nc.sync.dma_start(
+            out=w_sb[:].rearrange("p t c -> p (t c)"),
+            in_=w_qk.rearrange("(p t) c -> p (t c)", t=4),
+        )
+        x_sbs = []
+        for b, t_b in enumerate(BLOCK_T):
+            x_sb = const.tile([P, t_b * D], BF16, name="x_sb%d" % b)
+            r0 = block_tile0[b] * P
+            nc.sync.dma_start(
+                out=x_sb[:],
+                in_=x_flat[r0:r0 + t_b * P, :].rearrange("(p j) k -> p (j k)", j=t_b),
+            )
+            x_sbs.append(x_sb)
+
+        ident = const.tile([P, P], F32)
+        make_identity(nc, ident[:])
+
+        w_grp = const.tile([P, D * 4], BF16, align_bytes=64)
+        nc.vector.tensor_copy(
+            out=w_grp[:].rearrange("p (c i t) -> p c t i", i=4, t=4),
+            in_=w_sb[:].rearrange("p t (c i) -> p c t i", i=4),
+        )
+        w_codes = const.tile([P, D], U32, align_bytes=64)
+        w_scales = const.tile([P, D], U8, align_bytes=64)
+        nc.vector.quantize_mx(out=w_codes[:].bitcast(FP8X4), scales=w_scales[:], in_=w_grp[:])
+
+        xts = {}
+        x_grps = {}
+        codes = {}
+        accs = {}
+        u_pads = {}
+        prods = {}
+        rps = {}
+        ssums = {}
+        nrms = {}
+        o_tiles = {}
+
+        def transposes(k):
+            xt = ps_t.tile([P, 2, 2, P], F32, name="xt")
+            for jj in range(2):
+                i = 2 * k + jj
+                xw = x_sbs[tile_block[i]][:].bitcast(F32)
+                for u in range(2):
+                    c0 = tile_j[i] * 256
+                    nc.tensor.transpose(xt[:, jj, u, :], xw[:, c0 + u:c0 + 256:2], ident[:])
+            xts[k] = xt
+
+        def copy_out(k):
+            q = tile_q[2 * k]
+            if 2 * k == q_start[q]:
+                x_grps[q] = xq.tile([P, QUANT_TILES[q] * D], BF16, align_bytes=64, name="x_grp")
+            h = k - q_start[q] // 2
+            dst = x_grps[q][:].bitcast(F32)[:, h * 512:(h + 1) * 512].rearrange(
+                "p (j r u) -> p j r u", j=2, u=2)
+            src = xts[k][:].rearrange("p j u r -> p j r u")
+            if k in XT_ON_V:
+                nc.vector.tensor_copy(out=dst, in_=src)
+            else:
+                nc.scalar.copy(out=dst, in_=src)
+
+        def quantise(q):
+            n_q = QUANT_TILES[q]
+            x_codes = const.tile([P, n_q * P], U32, align_bytes=64, name="x_codes%d" % q)
+            x_scales = const.tile([P, n_q * P], U8, align_bytes=64, name="x_scales%d" % q)
+            nc.vector.quantize_mx(
+                out=x_codes[:].bitcast(FP8X4), scales=x_scales[:], in_=x_grps[q][:])
+            codes[q] = (x_codes, x_scales)
+
+        def project(i):
+            q = tile_q[i]
+            x_codes, x_scales = codes[q]
+            c0 = (i - q_start[q]) * P
+            acc = ps_a.tile([P, D], F32, name="acc")
+            nc.tensor.matmul_mx(
+                out=acc[:],
+                lhsT=x_codes[:, c0:c0 + P].bitcast(FP8X4),
+                lhsT_scale=x_scales[:, c0:c0 + P],
+                rhs=w_codes[:].bitcast(FP8X4),
+                rhs_scale=w_scales[:],
+                start=True,
+                stop=True,
+            )
+            accs[i] = acc[:].rearrange("p (g i) -> p g i", g=G)
+
+        def stage_up(i):
+            u_pad = work.tile([P, G, PADW], F32, name="u_pad")
+            nc.scalar.copy(out=u_pad[:, :, 4:PADW], in_=accs[i])
+            nc.scalar.activation(
+                out=u_pad[:, :, 3:4], in_=accs[i][:, :, DH - 1:DH], func=ACT.Copy, scale=-1.0)
+            u_pads[i] = u_pad
+
+        def stage_p(i):
+            prod = work.tile([P, G, DH], F32, name="prod")
+            nc.vector.tensor_tensor(
+                out=prod[:], in0=accs[i], in1=u_pads[i][:, :, 3:PADW - 1], op=ALU.mult)
+            prods[i] = prod
+
+        def stage_sum(i):
+            rp = work.tile([P, G, DH], F32, name="rp")
+            ssum = small.tile([P, G], F32, name="ssum")
+            for g in range(G):
+                nc.scalar.activation(
+                    out=rp[:, g, :], in_=prods[i][:, g, :], func=ACT.Relu,
+                    accum_out=ssum[:, g:g + 1])
+            rps[i] = rp
+            ssums[i] = ssum
+
+        def stage_norm(i):
+            rinv = small.tile([P, G], F32, name="rinv")
+            nc.vector.reciprocal(rinv[:], ssums[i][:])
+            nrm = work.tile([P, G, DH], F32, name="nrm")
+            m_eng = nc.vector if i in M_ON_V else nc.gpsimd
+            m_eng.tensor_tensor(
+                out=nrm[:], in0=rps[i][:], in1=rinv[:].unsqueeze(2).to_broadcast([P, G, DH]),
+                op=ALU.mult)
+            nrms[i] = nrm
+
+        def stage_out(i):
+            b = tile_block[i]
+            j = tile_j[i]
+            t_b = BLOCK_T[b]
+            if j == 0:
+                o_tiles[b] = outp.tile([P, G * t_b, 2 * DH], F32, name="o_sb")
+            o_sb = o_tiles[b]
+            o_view = o_sb[:].rearrange("p (g j) f -> p g j f", j=t_b)
+            nc.vector.scalar_tensor_tensor(
+                out=o_view[:, :, j, 0:DH], in0=accs[i], scalar=0.0, in1=nrms[i][:],
+                op0=ALU.is_gt, op1=ALU.mult)
+            if i in NEG_ON_G:
+                nc.gpsimd.tensor_tensor(
+                    out=o_view[:, :, j, DH:2 * DH], in0=nrms[i][:], in1=o_view[:, :, j, 0:DH],
+                    op=ALU.subtract)
+            else:
+                nc.vector.scalar_tensor_tensor(
+                    out=o_view[:, :, j, DH:2 * DH], in0=accs[i], scalar=0.0, in1=nrms[i][:],
+                    op0=ALU.is_lt, op1=ALU.mult)
+
+        def store(b):
+            t_b = BLOCK_T[b]
+            tok0 = block_tile0[b] * P
+            bb = tok0 // SEQ
+            n0 = tok0 % SEQ
+            half = (G // 2) * t_b
+            for dst, lo in ((out_0, 0), (out_1, half)):
+                nc.sync.dma_start(
+                    out=dst[bb, :, n0:n0 + t_b * P, :].rearrange("h (p j) f -> p h (j f)", j=t_b),
+                    in_=o_tiles[b][:, lo:lo + half, :].rearrange("p (h j) f -> p h (j f)", j=t_b),
+                )
+
+        for k in range(NT // 2):
+            if COPY_STEP[k] < 0:
+                transposes(k)
+                copy_out(k)
+        for q in range(len(QUANT_TILES)):
+            if QUANT_STEP[q] < 0:
+                quantise(q)
+        project(0)
+        for n in range(NT + OUT_LAG):
+            for k in range(NT // 2):
+                if COPY_STEP[k] == n:
+                    transposes(k)
+            if n + 1 < NT:
+                project(n + 1)
+            if 0 <= n - 2 < NT:
+                stage_norm(n - 2)
+            if n < NT:
+                stage_up(n)
+            if 0 <= n - OUT_LAG < NT:
+                stage_out(n - OUT_LAG)
+            if 0 <= n - 1 < NT:
+                stage_sum(n - 1)
+            if n < NT:
+                stage_p(n)
+            for k in range(NT // 2):
+                if COPY_STEP[k] == n:
+                    copy_out(k)
+            for q in range(len(QUANT_TILES)):
+                if QUANT_STEP[q] == n:
+                    quantise(q)
+            i = n - OUT_LAG
+            if 0 <= i < NT and tile_j[i] == BLOCK_T[tile_block[i]] - 1:
+                store(tile_block[i])

@@ -20,13 +20,15 @@ G = 8
 DH = 64
 PADW = 68
 BLOCK_T = (2, 2, 4, 4, 4, 4, 4, 2, 2, 2, 1, 1)
-QUANT_TILES = (2, 2, 4, 8, 8, 8)
-COPY_STEP = (-1, -1, 0, 0, 1, 2, 3, 4, 6, 8, 10, 12, 14, 16, 18, 20)
-QUANT_STEP = (-1, -1, 2, 6, 14, 22)
-XT_ON_V = (1, 2, 3, 4, 5)
-NEG_ON_G = ()
+QUANT_TILES = (2, 2, 4, 4, 4, 4, 4, 4, 4)
+COPY_LEAD = 6
+QUANT_LEAD = 3
+XT_ON_V = (1, 2, 3, 4)
 M_ON_V = (30, 31)
-OUT_LAG = 3
+P_LAG = 1
+SUM_LAG = 2
+NORM_LAG = 3
+OUT_LAG = 4
 
 FLOPS = 2 * TOKENS * D * D
 
@@ -188,14 +190,9 @@ def tile_dpfpattention_pa_t_kernel(tc, x, w_qk, out_0, out_1):
             nc.vector.scalar_tensor_tensor(
                 out=o_view[:, :, j, 0:DH], in0=accs[i], scalar=0.0, in1=nrms[i][:],
                 op0=ALU.is_gt, op1=ALU.mult)
-            if i in NEG_ON_G:
-                nc.gpsimd.tensor_tensor(
-                    out=o_view[:, :, j, DH:2 * DH], in0=nrms[i][:], in1=o_view[:, :, j, 0:DH],
-                    op=ALU.subtract)
-            else:
-                nc.vector.scalar_tensor_tensor(
-                    out=o_view[:, :, j, DH:2 * DH], in0=accs[i], scalar=0.0, in1=nrms[i][:],
-                    op0=ALU.is_lt, op1=ALU.mult)
+            nc.vector.scalar_tensor_tensor(
+                out=o_view[:, :, j, DH:2 * DH], in0=accs[i], scalar=0.0, in1=nrms[i][:],
+                op0=ALU.is_lt, op1=ALU.mult)
 
         def store(b):
             t_b = BLOCK_T[b]
@@ -209,36 +206,39 @@ def tile_dpfpattention_pa_t_kernel(tc, x, w_qk, out_0, out_1):
                     in_=o_tiles[b][:, lo:lo + half, :].rearrange("p (h j) f -> p h (j f)", j=t_b),
                 )
 
+        copy_step = [max(-1, 2 * k - COPY_LEAD) for k in range(NT // 2)]
+        quant_step = [max(-1, q_start[q] - QUANT_LEAD) for q in range(len(QUANT_TILES))]
+
         for k in range(NT // 2):
-            if COPY_STEP[k] < 0:
+            if copy_step[k] < 0:
                 transposes(k)
                 copy_out(k)
-        for q in range(len(QUANT_TILES)):
-            if QUANT_STEP[q] < 0:
-                quantise(q)
+            for q in range(len(QUANT_TILES)):
+                if quant_step[q] < 0 and q_start[q] + QUANT_TILES[q] == 2 * k + 2:
+                    quantise(q)
         project(0)
         for n in range(NT + OUT_LAG):
             for k in range(NT // 2):
-                if COPY_STEP[k] == n:
+                if copy_step[k] == n:
                     transposes(k)
             if n + 1 < NT:
                 project(n + 1)
-            if 0 <= n - 2 < NT:
-                stage_norm(n - 2)
             if n < NT:
                 stage_up(n)
+            if 0 <= n - P_LAG < NT:
+                stage_p(n - P_LAG)
+            for q in range(len(QUANT_TILES)):
+                if quant_step[q] == n:
+                    quantise(q)
+            if 0 <= n - NORM_LAG < NT:
+                stage_norm(n - NORM_LAG)
+            if 0 <= n - SUM_LAG < NT:
+                stage_sum(n - SUM_LAG)
             if 0 <= n - OUT_LAG < NT:
                 stage_out(n - OUT_LAG)
-            if 0 <= n - 1 < NT:
-                stage_sum(n - 1)
-            if n < NT:
-                stage_p(n)
             for k in range(NT // 2):
-                if COPY_STEP[k] == n:
+                if copy_step[k] == n:
                     copy_out(k)
-            for q in range(len(QUANT_TILES)):
-                if QUANT_STEP[q] == n:
-                    quantise(q)
             i = n - OUT_LAG
             if 0 <= i < NT and tile_j[i] == BLOCK_T[tile_block[i]] - 1:
                 store(tile_block[i])

@@ -18,13 +18,14 @@ SEQ = 2048
 NT = TOKENS // P
 G = 8
 DH = 64
-PADW = 68
+HALF = DH // 2
+PADW = HALF + 1
 BLOCK_T = (2, 2, 4, 4, 4, 4, 4, 2, 2, 2, 1, 1)
 QUANT_TILES = (2, 2, 4, 4, 4, 4, 4, 4, 4)
 COPY_LEAD = 6
 QUANT_LEAD = 3
-XT_ON_V = (1, 2, 3, 4)
-M_ON_V = (30, 31)
+XT_ON_V = (1, 2)
+M_ON_V = (31,)
 P_LAG = 1
 SUM_LAG = 2
 NORM_LAG = 3
@@ -92,7 +93,7 @@ def tile_dpfpattention_pa_t_kernel(tc, x, w_qk, out_0, out_1):
         x_grps = {}
         codes = {}
         accs = {}
-        u_pads = {}
+        odds = {}
         prods = {}
         rps = {}
         ssums = {}
@@ -147,16 +148,18 @@ def tile_dpfpattention_pa_t_kernel(tc, x, w_qk, out_0, out_1):
             accs[i] = acc[:].rearrange("p (g i) -> p g i", g=G)
 
         def stage_up(i):
-            u_pad = work.tile([P, G, PADW], F32, name="u_pad")
-            nc.scalar.copy(out=u_pad[:, :, 4:PADW], in_=accs[i])
+            odd = work.tile([P, G, PADW], F32, name="odd")
+            nc.scalar.copy(out=odd[:, :, 1:PADW], in_=accs[i][:, :, 1:DH:2])
             nc.scalar.activation(
-                out=u_pad[:, :, 3:4], in_=accs[i][:, :, DH - 1:DH], func=ACT.Copy, scale=-1.0)
-            u_pads[i] = u_pad
+                out=odd[:, :, 0:1], in_=accs[i][:, :, DH - 1:DH], func=ACT.Copy, scale=-1.0)
+            odds[i] = odd
 
         def stage_p(i):
-            prod = work.tile([P, G, DH], F32, name="prod")
-            nc.vector.tensor_tensor(
-                out=prod[:], in0=accs[i], in1=u_pads[i][:, :, 3:PADW - 1], op=ALU.mult)
+            prod = work.tile([P, 2, G, HALF], F32, name="prod")
+            even = accs[i][:, :, 0:DH:2]
+            for e in range(2):
+                nc.vector.tensor_tensor(
+                    out=prod[:, e, :, :], in0=even, in1=odds[i][:, :, e:e + HALF], op=ALU.mult)
             prods[i] = prod
 
         def stage_sum(i):
@@ -164,7 +167,8 @@ def tile_dpfpattention_pa_t_kernel(tc, x, w_qk, out_0, out_1):
             ssum = small.tile([P, G], F32, name="ssum")
             for g in range(G):
                 nc.scalar.activation(
-                    out=rp[:, g, :], in_=prods[i][:, g, :], func=ACT.Relu,
+                    out=rp[:, g, :].rearrange("p (i e) -> p i e", e=2),
+                    in_=prods[i][:, :, g, :].rearrange("p e i -> p i e"), func=ACT.Relu,
                     accum_out=ssum[:, g:g + 1])
             rps[i] = rp
             ssums[i] = ssum

from contextlib import ExitStack

import concourse.mybir as mybir
from concourse.masks import make_identity

F32 = mybir.dt.float32
BF16 = mybir.dt.bfloat16
U32 = mybir.dt.uint32
U8 = mybir.dt.uint8
FP8X4 = mybir.dt.float8_e4m3fn_x4
ALU = mybir.AluOpType
ACT = mybir.ActivationFunctionType

P = 128
D = 512
TOKENS = 4096
SEQ = 2048
NT = TOKENS // P
G = 8
DH = 64
HALF = DH // 2
PADW = HALF + 1
BLOCK_T = (2, 2, 4, 4, 4, 4, 4, 2, 2, 2, 1, 1)
QUANT_TILES = (2, 2, 4, 4, 4, 4, 4, 4, 4)
COPY_LEAD = 6
QUANT_LEAD = 3
XT_ON_V = (1, 2)
M_ON_V = (31,)
P_LAG = 1
SUM_LAG = 2
NORM_LAG = 3
OUT_LAG = 4

FLOPS = 2 * TOKENS * D * D


def tile_dpfpattention_pa_t_kernel(tc, x, w_qk, out_0, out_1):
    nc = tc.nc
    x_flat = x.flatten_outer_dims()
    tile_block = []
    tile_j = []
    block_tile0 = []
    for b, t_b in enumerate(BLOCK_T):
        block_tile0.append(len(tile_block))
        for j in range(t_b):
            tile_block.append(b)
            tile_j.append(j)
    assert len(tile_block) == NT
    q_start = [sum(QUANT_TILES[:q]) for q in range(len(QUANT_TILES))]
    assert sum(QUANT_TILES) == NT
    tile_q = []
    for q, n_q in enumerate(QUANT_TILES):
        tile_q.extend([q] * n_q)

    with ExitStack() as ctx:
        const = ctx.enter_context(tc.tile_pool(name="const", bufs=1))
        xq = ctx.enter_context(tc.tile_pool(name="xq", bufs=2))
        work = ctx.enter_context(tc.tile_pool(name="work", bufs=4))
        small = ctx.enter_context(tc.tile_pool(name="small", bufs=8))
        outp = ctx.enter_context(tc.tile_pool(name="outp", bufs=5))
        ps_t = ctx.enter_context(tc.psum_pool(name="ps_t", bufs=2))
        ps_a = ctx.enter_context(tc.psum_pool(name="ps_a", bufs=6))
        ctx.enter_context(tc.manual_schedule())

        w_sb = const.tile([P, 4, D], BF16)
        nc.sync.dma_start(
            out=w_sb[:].rearrange("p t c -> p (t c)"),
            in_=w_qk.rearrange("(p t) c -> p (t c)", t=4),
        )
        x_sbs = []
        for b, t_b in enumerate(BLOCK_T):
            x_sb = const.tile([P, t_b * D], BF16, name="x_sb%d" % b)
            r0 = block_tile0[b] * P
            nc.sync.dma_start(
                out=x_sb[:],
                in_=x_flat[r0:r0 + t_b * P, :].rearrange("(p j) k -> p (j k)", j=t_b),
            )
            x_sbs.append(x_sb)

        ident = const.tile([P, P], F32)
        make_identity(nc, ident[:])

        w_grp = const.tile([P, D * 4], BF16, align_bytes=64)
        nc.vector.tensor_copy(
            out=w_grp[:].rearrange("p (c i t) -> p c t i", i=4, t=4),
            in_=w_sb[:].rearrange("p t (c i) -> p c t i", i=4),
        )
        w_codes = const.tile([P, D], U32, align_bytes=64)
        w_scales = const.tile([P, D], U8, align_bytes=64)
        nc.vector.quantize_mx(out=w_codes[:].bitcast(FP8X4), scales=w_scales[:], in_=w_grp[:])

        xts = {}
        x_grps = {}
        codes = {}
        accs = {}
        odds = {}
        prods = {}
        rps = {}
        ssums = {}
        nrms = {}
        o_tiles = {}

        def transposes(k):
            xt = ps_t.tile([P, 2, 2, P], F32, name="xt")
            for jj in range(2):
                i = 2 * k + jj
                xw = x_sbs[tile_block[i]][:].bitcast(F32)
                for u in range(2):
                    c0 = tile_j[i] * 256
                    nc.tensor.transpose(xt[:, jj, u, :], xw[:, c0 + u:c0 + 256:2], ident[:])
            xts[k] = xt

        def copy_out(k):
            q = tile_q[2 * k]
            if 2 * k == q_start[q]:
                x_grps[q] = xq.tile([P, QUANT_TILES[q] * D], BF16, align_bytes=64, name="x_grp")
            h = k - q_start[q] // 2
            dst = x_grps[q][:].bitcast(F32)[:, h * 512:(h + 1) * 512].rearrange(
                "p (j r u) -> p j r u", j=2, u=2)
            src = xts[k][:].rearrange("p j u r -> p j r u")
            if k in XT_ON_V:
                nc.vector.tensor_copy(out=dst, in_=src)
            else:
                nc.scalar.copy(out=dst, in_=src)

        def quantise(q):
            n_q = QUANT_TILES[q]
            x_codes = const.tile([P, n_q * P], U32, align_bytes=64, name="x_codes%d" % q)
            x_scales = const.tile([P, n_q * P], U8, align_bytes=64, name="x_scales%d" % q)
            nc.vector.quantize_mx(
                out=x_codes[:].bitcast(FP8X4), scales=x_scales[:], in_=x_grps[q][:])
            codes[q] = (x_codes, x_scales)

        def project(i):
            q = tile_q[i]
            x_codes, x_scales = codes[q]
            c0 = (i - q_start[q]) * P
            acc = ps_a.tile([P, D], F32, name="acc")
            nc.tensor.matmul_mx(
                out=acc[:],
                lhsT=x_codes[:, c0:c0 + P].bitcast(FP8X4),
                lhsT_scale=x_scales[:, c0:c0 + P],
                rhs=w_codes[:].bitcast(FP8X4),
                rhs_scale=w_scales[:],
                start=True,
                stop=True,
            )
            accs[i] = acc[:].rearrange("p (g i) -> p g i", g=G)

        def stage_up(i):
            odd = work.tile([P, G, PADW], F32, name="odd")
            nc.scalar.copy(out=odd[:, :, 1:PADW], in_=accs[i][:, :, 1:DH:2])
            nc.scalar.activation(
                out=odd[:, :, 0:1], in_=accs[i][:, :, DH - 1:DH], func=ACT.Copy, scale=-1.0)
            odds[i] = odd

        def stage_p(i):
            prod = work.tile([P, 2, G, HALF], F32, name="prod")
            even = accs[i][:, :, 0:DH:2]
            for e in range(2):
                nc.vector.tensor_tensor(
                    out=prod[:, e, :, :], in0=even, in1=odds[i][:, :, e:e + HALF], op=ALU.mult)
            prods[i] = prod

        def stage_sum(i):
            rp = work.tile([P, G, DH], F32, name="rp")
            ssum = small.tile([P, G], F32, name="ssum")
            for g in range(G):
                nc.scalar.activation(
                    out=rp[:, g, :].rearrange("p (i e) -> p i e", e=2),
                    in_=prods[i][:, :, g, :].rearrange("p e i -> p i e"), func=ACT.Relu,
                    accum_out=ssum[:, g:g + 1])
            rps[i] = rp
            ssums[i] = ssum

        def stage_norm(i):
            rinv = small.tile([P, G], F32, name="rinv")
            nc.vector.reciprocal(rinv[:], ssums[i][:])
            nrm = work.tile([P, G, DH], F32, name="nrm")
            m_eng = nc.vector if i in M_ON_V else nc.gpsimd
            m_eng.tensor_tensor(
                out=nrm[:], in0=rps[i][:], in1=rinv[:].unsqueeze(2).to_broadcast([P, G, DH]),
                op=ALU.mult)
            nrms[i] = nrm

        def stage_out(i):
            b = tile_block[i]
            j = tile_j[i]
            t_b = BLOCK_T[b]
            if j == 0:
                o_tiles[b] = outp.tile([P, G * t_b, 2 * DH], F32, name="o_sb")
            o_sb = o_tiles[b]
            o_view = o_sb[:].rearrange("p (g j) f -> p g j f", j=t_b)
            nc.vector.scalar_tensor_tensor(
                out=o_view[:, :, j, 0:DH], in0=accs[i], scalar=0.0, in1=nrms[i][:],
                op0=ALU.is_gt, op1=ALU.mult)
            nc.vector.scalar_tensor_tensor(
                out=o_view[:, :, j, DH:2 * DH], in0=accs[i], scalar=0.0, in1=nrms[i][:],
                op0=ALU.is_lt, op1=ALU.mult)

        def store(b):
            t_b = BLOCK_T[b]
            tok0 = block_tile0[b] * P
            bb = tok0 // SEQ
            n0 = tok0 % SEQ
            half = (G // 2) * t_b
            for dst, lo in ((out_0, 0), (out_1, half)):
                nc.sync.dma_start(
                    out=dst[bb, :, n0:n0 + t_b * P, :].rearrange("h (p j) f -> p h (j f)", j=t_b),
                    in_=o_tiles[b][:, lo:lo + half, :].rearrange("p (h j) f -> p h (j f)", j=t_b),
                )

        copy_step = [max(-1, 2 * k - COPY_LEAD) for k in range(NT // 2)]
        quant_step = [max(-1, q_start[q] - QUANT_LEAD) for q in range(len(QUANT_TILES))]

        for k in range(NT // 2):
            if copy_step[k] < 0:
                transposes(k)
                copy_out(k)
            for q in range(len(QUANT_TILES)):
                if quant_step[q] < 0 and q_start[q] + QUANT_TILES[q] == 2 * k + 2:
                    quantise(q)
        project(0)
        for n in range(NT + OUT_LAG):
            for k in range(NT // 2):
                if copy_step[k] == n:
                    transposes(k)
            if n + 1 < NT:
                project(n + 1)
            if n < NT:
                stage_up(n)
            if 0 <= n - P_LAG < NT:
                stage_p(n - P_LAG)
            for q in range(len(QUANT_TILES)):
                if quant_step[q] == n:
                    quantise(q)
            if 0 <= n - NORM_LAG < NT:
                stage_norm(n - NORM_LAG)
            if 0 <= n - SUM_LAG < NT:
                stage_sum(n - SUM_LAG)
            if 0 <= n - OUT_LAG < NT:
                stage_out(n - OUT_LAG)
            for k in range(NT // 2):
                if copy_step[k] == n:
                    copy_out(k)
            i = n - OUT_LAG
            if 0 <= i < NT and tile_j[i] == BLOCK_T[tile_block[i]] - 1:
                store(tile_block[i])
